import numpy as np
import ml_dtypes


def mxq(x, axis, fmt="e4m3"):
    dtype, down = {"e4m3": (ml_dtypes.float8_e4m3fn, 7), "e5m2": (ml_dtypes.float8_e5m2, 14)}[fmt]
    v = np.moveaxis(np.asarray(x, np.float32).astype(ml_dtypes.bfloat16).astype(np.float64), axis, -1)
    blocks = v.reshape(v.shape[:-1] + (-1, 32))
    amax = np.abs(blocks).max(-1, keepdims=True)
    byte = np.maximum(np.where(amax > 0, np.frexp(amax)[1] - 1 + 127, 0) - down, 1)
    scale = np.exp2(byte - 127.0)
    codes = (blocks / scale).astype(np.float32).astype(dtype).astype(np.float64)
    return np.moveaxis((codes * scale).reshape(v.shape), -1, axis)


WIDE = False


def mx_kscale(k):
    if not WIDE:
        return np.ones(k)
    levels = np.array([10, -10, 5, -5, 0])
    a = np.random.permutation(np.resize(levels, k // 512 * 4)).reshape(k // 512, 4)
    idx = np.arange(k)
    return np.exp2(a[idx // 512, idx % 128 // 32])


BF16 = ml_dtypes.bfloat16


def bf(x):
    return np.asarray(x, np.float32).astype(BF16)


def f64(x):
    return np.asarray(x).astype(np.float64)


E2M1 = np.array([0.0, 0.5, 1.0, 1.5, 2.0, 3.0, 4.0, 6.0, -0.0, -0.5, -1.0, -1.5, -2.0, -3.0, -4.0, -6.0])


def pack_weight(w, fmt):
    k, n = w.shape
    w = f64(bf(w)).reshape(k // 32, 32, n)
    amax = np.abs(w).max(1)
    if fmt == "e4m3":
        byte = np.frexp(amax)[1] - 1 + 127 - 7
    else:
        mant, ex = np.frexp(amax / 6.0)
        byte = np.where(mant > 0.5, ex, ex - 1) + 127
    byte = np.clip(np.where(amax > 0, byte, 1), 1, 254)
    scaled = (w * np.exp2(127.0 - byte)[:, None, :]).reshape(k, n).astype(np.float32)
    by_word = np.ascontiguousarray(scaled.reshape(k // 512, 128, 4, n).transpose(0, 1, 3, 2))
    if fmt == "e4m3":
        words = by_word.astype(ml_dtypes.float8_e4m3fn).view(np.uint8)
    else:
        c = by_word.astype(ml_dtypes.float4_e2m1fn).view(np.uint8) & 0xF
        words = c[..., 0::2] | (c[..., 1::2] << 4)
    return np.ascontiguousarray(words), np.ascontiguousarray(byte.astype(np.uint8).reshape(k // 512, 16, n))


def unpack_weight(words, scales, fmt):
    g, p, n, _ = words.shape
    if fmt == "e4m3":
        vals = np.ascontiguousarray(words).view(ml_dtypes.float8_e4m3fn).astype(np.float64)
    else:
        nib = np.empty((g, p, n, 4), np.uint8)
        nib[..., 0::2] = words & 0xF
        nib[..., 1::2] = words >> 4
        vals = E2M1[nib]
    vals = vals * np.repeat(np.exp2(scales.astype(np.float64) - 127.0), 8, axis=1)[..., None]
    return vals.transpose(0, 1, 3, 2).reshape(g * 512, n)

def pack4(w):
    words, scales = pack_weight(w, "e2m1")
    return words.reshape(words.shape[0], 128, -1), scales


def unpack4(words, scales):
    return unpack_weight(words.reshape(words.shape[0], 128, -1, 2), scales, "e2m1")


B, S, D, BD, K = 4, 128, 512, 512, 128
TS = 3.0


def sigmoid(v):
    return 1.0 / (1.0 + np.exp(-v))


def setup_inputs():
    s = mx_kscale(D)
    token_embeddings = bf(np.random.standard_normal((B, S, D)) * TS * s)
    splat_influences = bf(np.random.uniform(size=(B, S, K)))
    decoded = bf(np.random.standard_normal((B, K, D)) * 0.35)
    gate_W_words, gate_W_scales = pack4(np.random.standard_normal((D, D)) / (TS * np.sqrt(D)) / s[:, None])
    gate_b = bf(np.random.standard_normal(D) * 0.5)
    return {
        "token_embeddings": token_embeddings,
        "splat_influences": splat_influences,
        "decoded": decoded,
        "gate_W_words": gate_W_words,
        "gate_W_scales": gate_W_scales,
        "gate_b": gate_b,
    }


def reference(token_embeddings, splat_influences, decoded, gate_W_words, gate_W_scales, gate_b):
    flow = f64(splat_influences) @ f64(decoded)
    gate = sigmoid((mxq(f64(token_embeddings), 2, "e4m3") @ unpack4(gate_W_words, gate_W_scales)) + f64(gate_b))
    return flow * gate

@@ -1,0 +1,112 @@
+from contextlib import ExitStack
+
+import concourse.mybir as mybir
+from concourse.masks import make_identity
+
+F32 = mybir.dt.float32
+BF16 = mybir.dt.bfloat16
+I32 = mybir.dt.int32
+U32 = mybir.dt.uint32
+U8 = mybir.dt.uint8
+FP8X4 = mybir.dt.float8_e4m3fn_x4
+FP4X4 = mybir.dt.float4_e2m1fn_x4
+SIGMOID = mybir.ActivationFunctionType.Sigmoid
+
+P = 128
+PACK = 4
+B = 4
+TOKENS = 128
+SPLATS = 128
+D = 512
+WORDS = 2
+PSUM_BANKS = 8
+
+FLOPS = 2 * B * TOKENS * D * D + 2 * B * TOKENS * SPLATS * D
+
+
+def tile_splatinformationflow_pb_s_kernel(
+    tc, token_embeddings, splat_influences, decoded, gate_W_words, gate_W_scales, gate_b, out
+):
+    nc = tc.nc
+    with ExitStack() as ctx:
+        keep = ctx.enter_context(tc.tile_pool(name="keep", bufs=1))
+        psum = ctx.enter_context(tc.psum_pool(name="psum", bufs=PSUM_BANKS))
+
+        bias_rows = keep.tile([P, D], BF16)
+        nc.vector.memset(bias_rows[:], 0.0)
+        ones = keep.tile([P, P], BF16)
+        nc.vector.memset(ones[:], 1.0)
+        w_scales = keep.tile([P, D], U8, align_bytes=64)
+        nc.vector.memset(w_scales[:].bitcast(I32), 0)
+        scratch = keep.tile([P, 1], F32)
+        nc.vector.memset(scratch[:], 0.0)
+        ident_f32 = keep.tile([P, P], F32)
+        make_identity(nc, ident_f32[:])
+        ident_bf16 = keep.tile([P, P], BF16)
+        make_identity(nc, ident_bf16[:])
+
+        x_sb = [keep.tile([P, D], BF16, name="x%d" % b) for b in range(B)]
+        infl_sb = keep.tile([P, B, SPLATS], BF16)
+        w_words = keep.tile([P, 2 * D], U8, align_bytes=64)
+        dec_sb = [keep.tile([P, 2, D], BF16, name="dec%d" % h) for h in range(B // 2)]
+
+        nc.sync.dma_start(out=x_sb[0][:], in_=token_embeddings[0])
+        nc.sync.dma_start(out=bias_rows[0:1, :], in_=gate_b.unsqueeze(0))
+        for b in range(1, B):
+            nc.sync.dma_start(out=x_sb[b][:], in_=token_embeddings[b])
+        nc.sync.dma_start(out=w_words[:].bitcast(I32), in_=gate_W_words[0].bitcast(I32))
+        for q in range(P // 32):
+            nc.sync.dma_start(
+                out=w_scales[32 * q : 32 * q + 4, :].bitcast(I32),
+                in_=gate_W_scales[0, 4 * q : 4 * q + 4, :].bitcast(I32),
+            )
+        nc.sync.dma_start(out=infl_sb[:], in_=splat_influences.rearrange("b s k -> s b k"))
+        for h in range(B // 2):
+            nc.sync.dma_start(out=dec_sb[h][:], in_=decoded[2 * h : 2 * h + 2].rearrange("b k d -> k b d"))
+
+        nc.scalar.activation(out=scratch[:], in_=scratch[:], func=SIGMOID)
+
+        x_codes = [keep.tile([P, TOKENS], U32, name="x_codes%d" % b, align_bytes=64) for b in range(B)]
+        x_scales = [keep.tile([P, TOKENS], U8, name="x_scales%d" % b, align_bytes=64) for b in range(B)]
+        for b in range(B):
+            x_words = x_sb[b][:].bitcast(F32)
+            xT = psum.tile([P, WORDS, TOKENS], F32, tag="bank")
+            for u in range(WORDS):
+                nc.tensor.transpose(xT[:, u, :], x_words[:, u : D // 2 : WORDS], ident_f32[:])
+            grouped = keep.tile([P, TOKENS * PACK], BF16, name="grouped%d" % b, align_bytes=64)
+            nc.scalar.copy(
+                out=grouped[:].bitcast(F32).rearrange("p (s u) -> p s u", u=WORDS),
+                in_=xT[:].rearrange("p u s -> p s u"),
+            )
+            nc.vector.quantize_mx(out=x_codes[b][:].bitcast(FP8X4), scales=x_scales[b][:], in_=grouped[:])
+
+        bias_ps = psum.tile([P, D], F32, tag="bank")
+        nc.tensor.matmul(out=bias_ps[:], lhsT=ones[:], rhs=bias_rows[:], start=True, stop=True)
+        bias_all = keep.tile([P, D], F32)
+        nc.vector.tensor_copy(out=bias_all[:], in_=bias_ps[:])
+
+        inflT_ps = psum.tile([P, B, TOKENS], BF16, tag="bank")
+        for b in range(B):
+            nc.tensor.transpose(inflT_ps[:, b, :], infl_sb[:, b, :], ident_bf16[:])
+        inflT = keep.tile([P, B, TOKENS], BF16)
+        nc.scalar.copy(out=inflT[:], in_=inflT_ps[:])
+
+        for b in range(B):
+            gate_ps = psum.tile([P, D], F32, tag="bank")
+            nc.tensor.matmul_mx(
+                out=gate_ps[:],
+                lhsT=x_codes[b][:].bitcast(FP8X4),
+                lhsT_scale=x_scales[b][:],
+                rhs=w_words[:].bitcast(FP4X4),
+                rhs_scale=w_scales[:],
+                start=True,
+                stop=True,
+            )
+            flow_ps = psum.tile([P, D], F32, tag="bank")
+            nc.tensor.matmul(out=flow_ps[:], lhsT=inflT[:, b, :], rhs=dec_sb[b // 2][:, b % 2, :], start=True, stop=True)
+            gate = keep.tile([P, D], F32, name="gate%d" % b)
+            nc.vector.tensor_add(out=gate[:], in0=gate_ps[:], in1=bias_all[:])
+            nc.scalar.activation(out=gate[:], in_=gate[:], func=SIGMOID)
+            result = keep.tile([P, D], F32, name="result%d" % b)
+            nc.vector.tensor_mul(out=result[:], in0=gate[:], in1=flow_ps[:])
+            nc.sync.dma_start(out=out[b], in_=result[:])

@@ -20,6 +20,7 @@ SPLATS = 128
 D = 512
 WORDS = 2
 PSUM_BANKS = 8
+AHEAD = 2
 
 FLOPS = 2 * B * TOKENS * D * D + 2 * B * TOKENS * SPLATS * D
 
@@ -31,13 +32,14 @@ def tile_splatinformationflow_pb_s_kernel(
     with ExitStack() as ctx:
         keep = ctx.enter_context(tc.tile_pool(name="keep", bufs=1))
         psum = ctx.enter_context(tc.psum_pool(name="psum", bufs=PSUM_BANKS))
+        ctx.enter_context(tc.manual_schedule())
 
         bias_rows = keep.tile([P, D], BF16)
         nc.vector.memset(bias_rows[:], 0.0)
-        ones = keep.tile([P, P], BF16)
-        nc.vector.memset(ones[:], 1.0)
         w_scales = keep.tile([P, D], U8, align_bytes=64)
         nc.vector.memset(w_scales[:].bitcast(I32), 0)
+        ones = keep.tile([P, P], BF16)
+        nc.vector.memset(ones[:], 1.0)
         scratch = keep.tile([P, 1], F32)
         nc.vector.memset(scratch[:], 0.0)
         ident_f32 = keep.tile([P, P], F32)
@@ -45,15 +47,16 @@ def tile_splatinformationflow_pb_s_kernel(
         ident_bf16 = keep.tile([P, P], BF16)
         make_identity(nc, ident_bf16[:])
 
-        x_sb = [keep.tile([P, D], BF16, name="x%d" % b) for b in range(B)]
+        x_first = keep.tile([P, D], BF16)
+        x_rest = keep.tile([P, B - 1, D], BF16)
+        x_sb = [x_first[:]] + [x_rest[:, b - 1, :] for b in range(1, B)]
         infl_sb = keep.tile([P, B, SPLATS], BF16)
         w_words = keep.tile([P, 2 * D], U8, align_bytes=64)
         dec_sb = [keep.tile([P, 2, D], BF16, name="dec%d" % h) for h in range(B // 2)]
 
-        nc.sync.dma_start(out=x_sb[0][:], in_=token_embeddings[0])
+        nc.sync.dma_start(out=x_first[:], in_=token_embeddings[0])
         nc.sync.dma_start(out=bias_rows[0:1, :], in_=gate_b.unsqueeze(0))
-        for b in range(1, B):
-            nc.sync.dma_start(out=x_sb[b][:], in_=token_embeddings[b])
+        nc.sync.dma_start(out=x_rest[:], in_=token_embeddings[1:B].rearrange("b s d -> s b d"))
         nc.sync.dma_start(out=w_words[:].bitcast(I32), in_=gate_W_words[0].bitcast(I32))
         for q in range(P // 32):
             nc.sync.dma_start(
@@ -68,8 +71,9 @@ def tile_splatinformationflow_pb_s_kernel(
 
         x_codes = [keep.tile([P, TOKENS], U32, name="x_codes%d" % b, align_bytes=64) for b in range(B)]
         x_scales = [keep.tile([P, TOKENS], U8, name="x_scales%d" % b, align_bytes=64) for b in range(B)]
-        for b in range(B):
-            x_words = x_sb[b][:].bitcast(F32)
+
+        def quantise_tokens(b):
+            x_words = x_sb[b].bitcast(F32)
             xT = psum.tile([P, WORDS, TOKENS], F32, tag="bank")
             for u in range(WORDS):
                 nc.tensor.transpose(xT[:, u, :], x_words[:, u : D // 2 : WORDS], ident_f32[:])
@@ -80,21 +84,21 @@ def tile_splatinformationflow_pb_s_kernel(
             )
             nc.vector.quantize_mx(out=x_codes[b][:].bitcast(FP8X4), scales=x_scales[b][:], in_=grouped[:])
 
+        quantise_tokens(0)
+
         bias_ps = psum.tile([P, D], F32, tag="bank")
         nc.tensor.matmul(out=bias_ps[:], lhsT=ones[:], rhs=bias_rows[:], start=True, stop=True)
         bias_all = keep.tile([P, D], F32)
         nc.vector.tensor_copy(out=bias_all[:], in_=bias_ps[:])
 
-        inflT_ps = psum.tile([P, B, TOKENS], BF16, tag="bank")
-        for b in range(B):
-            nc.tensor.transpose(inflT_ps[:, b, :], infl_sb[:, b, :], ident_bf16[:])
-        inflT = keep.tile([P, B, TOKENS], BF16)
-        nc.scalar.copy(out=inflT[:], in_=inflT_ps[:])
+        for b in range(1, B):
+            quantise_tokens(b)
 
-        for b in range(B):
-            gate_ps = psum.tile([P, D], F32, tag="bank")
+        gate_ps = [psum.tile([P, D], F32, tag="bank", name="gate_ps%d" % b) for b in range(B)]
+
+        def gate_pass(b):
             nc.tensor.matmul_mx(
-                out=gate_ps[:],
+                out=gate_ps[b][:],
                 lhsT=x_codes[b][:].bitcast(FP8X4),
                 lhsT_scale=x_scales[b][:],
                 rhs=w_words[:].bitcast(FP4X4),
@@ -102,11 +106,31 @@ def tile_splatinformationflow_pb_s_kernel(
                 start=True,
                 stop=True,
             )
-            flow_ps = psum.tile([P, D], F32, tag="bank")
-            nc.tensor.matmul(out=flow_ps[:], lhsT=inflT[:, b, :], rhs=dec_sb[b // 2][:, b % 2, :], start=True, stop=True)
-            gate = keep.tile([P, D], F32, name="gate%d" % b)
-            nc.vector.tensor_add(out=gate[:], in0=gate_ps[:], in1=bias_all[:])
-            nc.scalar.activation(out=gate[:], in_=gate[:], func=SIGMOID)
-            result = keep.tile([P, D], F32, name="result%d" % b)
-            nc.vector.tensor_mul(out=result[:], in0=gate[:], in1=flow_ps[:])
-            nc.sync.dma_start(out=out[b], in_=result[:])
+
+        for b in range(B // 2):
+            gate_pass(b)
+        inflT_ps = psum.tile([P, B, TOKENS], BF16, tag="bank")
+        for b in range(B):
+            nc.tensor.transpose(inflT_ps[:, b, :], infl_sb[:, b, :], ident_bf16[:])
+        inflT = keep.tile([P, B, TOKENS], BF16)
+        nc.scalar.copy(out=inflT[:], in_=inflT_ps[:])
+        for b in range(B // 2, B):
+            gate_pass(b)
+
+        flow_ps = [psum.tile([P, D], F32, tag="bank", name="flow_ps%d" % b) for b in range(B)]
+        for b in range(B):
+            nc.tensor.matmul(
+                out=flow_ps[b][:], lhsT=inflT[:, b, :], rhs=dec_sb[b // 2][:, b % 2, :], start=True, stop=True
+            )
+
+        gate = [keep.tile([P, D], F32, name="gate%d" % b) for b in range(B)]
+        result = [keep.tile([P, D], F32, name="result%d" % b) for b in range(B)]
+        for step in range(B + AHEAD):
+            if step < B:
+                b = step
+                nc.vector.tensor_add(out=gate[b][:], in0=gate_ps[b][:], in1=bias_all[:])
+                nc.scalar.activation(out=gate[b][:], in_=gate[b][:], func=SIGMOID)
+            if step >= AHEAD:
+                b = step - AHEAD
+                nc.vector.tensor_mul(out=result[b][:], in0=gate[b][:], in1=flow_ps[b][:])
+                nc.sync.dma_start(out=out[b], in_=result[b][:])

@@ -20,7 +20,6 @@ SPLATS = 128
 D = 512
 WORDS = 2
 PSUM_BANKS = 8
-AHEAD = 2
 
 FLOPS = 2 * B * TOKENS * D * D + 2 * B * TOKENS * SPLATS * D
 
@@ -124,13 +123,10 @@ def tile_splatinformationflow_pb_s_kernel(
             )
 
         gate = [keep.tile([P, D], F32, name="gate%d" % b) for b in range(B)]
-        result = [keep.tile([P, D], F32, name="result%d" % b) for b in range(B)]
-        for step in range(B + AHEAD):
-            if step < B:
-                b = step
-                nc.vector.tensor_add(out=gate[b][:], in0=gate_ps[b][:], in1=bias_all[:])
-                nc.scalar.activation(out=gate[b][:], in_=gate[b][:], func=SIGMOID)
-            if step >= AHEAD:
-                b = step - AHEAD
-                nc.vector.tensor_mul(out=result[b][:], in0=gate[b][:], in1=flow_ps[b][:])
-                nc.sync.dma_start(out=out[b], in_=result[b][:])
+        for b in range(B):
+            nc.vector.tensor_add(out=gate[b][:], in0=gate_ps[b][:], in1=bias_all[:])
+            nc.scalar.activation(out=gate[b][:], in_=gate[b][:], func=SIGMOID)
+        for b in range(B):
+            result = keep.tile([P, D], F32, name="result%d" % b)
+            nc.vector.tensor_mul(out=result[:], in0=gate[b][:], in1=flow_ps[b][:])
+            nc.sync.dma_start(out=out[b], in_=result[:])

@@ -20,6 +20,7 @@ SPLATS = 128
 D = 512
 WORDS = 2
 PSUM_BANKS = 8
+WARM_UPS = 4
 
 FLOPS = 2 * B * TOKENS * D * D + 2 * B * TOKENS * SPLATS * D
 
@@ -33,12 +34,10 @@ def tile_splatinformationflow_pb_s_kernel(
         psum = ctx.enter_context(tc.psum_pool(name="psum", bufs=PSUM_BANKS))
         ctx.enter_context(tc.manual_schedule())
 
-        bias_rows = keep.tile([P, D], BF16)
-        nc.vector.memset(bias_rows[:], 0.0)
+        warm = keep.tile([P, P], F32)
+        nc.vector.memset(warm[:], 0.0)
         w_scales = keep.tile([P, D], U8, align_bytes=64)
         nc.vector.memset(w_scales[:].bitcast(I32), 0)
-        ones = keep.tile([P, P], BF16)
-        nc.vector.memset(ones[:], 1.0)
         scratch = keep.tile([P, 1], F32)
         nc.vector.memset(scratch[:], 0.0)
         ident_f32 = keep.tile([P, P], F32)
@@ -54,7 +53,8 @@ def tile_splatinformationflow_pb_s_kernel(
         dec_sb = [keep.tile([P, 2, D], BF16, name="dec%d" % h) for h in range(B // 2)]
 
         nc.sync.dma_start(out=x_first[:], in_=token_embeddings[0])
-        nc.sync.dma_start(out=bias_rows[0:1, :], in_=gate_b.unsqueeze(0))
+        bias_col = keep.tile([P, PACK], BF16)
+        nc.sync.dma_start(out=bias_col[:], in_=gate_b.rearrange("(p c) -> p c", c=PACK))
         nc.sync.dma_start(out=x_rest[:], in_=token_embeddings[1:B].rearrange("b s d -> s b d"))
         nc.sync.dma_start(out=w_words[:].bitcast(I32), in_=gate_W_words[0].bitcast(I32))
         for q in range(P // 32):
@@ -65,6 +65,10 @@ def tile_splatinformationflow_pb_s_kernel(
         nc.sync.dma_start(out=infl_sb[:], in_=splat_influences.rearrange("b s k -> s b k"))
         for h in range(B // 2):
             nc.sync.dma_start(out=dec_sb[h][:], in_=decoded[2 * h : 2 * h + 2].rearrange("b k d -> k b d"))
+
+        warm_ps = psum.tile([P, P], F32, tag="bank")
+        for i in range(WARM_UPS):
+            nc.tensor.matmul(out=warm_ps[:], lhsT=warm[:], rhs=warm[:], start=True, stop=True)
 
         nc.scalar.activation(out=scratch[:], in_=scratch[:], func=SIGMOID)
 
@@ -85,10 +89,15 @@ def tile_splatinformationflow_pb_s_kernel(
 
         quantise_tokens(0)
 
-        bias_ps = psum.tile([P, D], F32, tag="bank")
-        nc.tensor.matmul(out=bias_ps[:], lhsT=ones[:], rhs=bias_rows[:], start=True, stop=True)
-        bias_all = keep.tile([P, D], F32)
-        nc.vector.tensor_copy(out=bias_all[:], in_=bias_ps[:])
+        bias_ps = psum.tile([P, WORDS, P], F32, tag="bank")
+        bias_words = bias_col[:].bitcast(F32)
+        for u in range(WORDS):
+            nc.tensor.transpose(bias_ps[:, u, :], bias_words[:, u : u + 1].to_broadcast([P, P]), ident_f32[:])
+        bias_all = keep.tile([P, D], BF16)
+        nc.scalar.copy(
+            out=bias_all[:].bitcast(F32).rearrange("p (s u) -> p s u", u=WORDS),
+            in_=bias_ps[:].rearrange("p u s -> p s u"),
+        )
 
         for b in range(1, B):
             quantise_tokens(b)

@@ -35,33 +35,43 @@ def tile_splatinformationflow_pb_s_kernel(
         ctx.enter_context(tc.manual_schedule())
 
         warm = keep.tile([P, P], F32)
-        nc.vector.memset(warm[:], 0.0)
         w_scales = keep.tile([P, D], U8, align_bytes=64)
-        nc.vector.memset(w_scales[:].bitcast(I32), 0)
         scratch = keep.tile([P, 1], F32)
-        nc.vector.memset(scratch[:], 0.0)
         ident_f32 = keep.tile([P, P], F32)
-        make_identity(nc, ident_f32[:])
         ident_bf16 = keep.tile([P, P], BF16)
-        make_identity(nc, ident_bf16[:])
-
         x_first = keep.tile([P, D], BF16)
         x_rest = keep.tile([P, B - 1, D], BF16)
         x_sb = [x_first[:]] + [x_rest[:, b - 1, :] for b in range(1, B)]
         infl_sb = keep.tile([P, B, SPLATS], BF16)
         w_words = keep.tile([P, 2 * D], U8, align_bytes=64)
         dec_sb = [keep.tile([P, 2, D], BF16, name="dec%d" % h) for h in range(B // 2)]
+        bias_col = keep.tile([P, PACK], BF16)
+        bias_all = keep.tile([P, D], BF16)
+        inflT = keep.tile([P, B, TOKENS], BF16)
+        grouped = [keep.tile([P, TOKENS * PACK], BF16, name="grouped%d" % b, align_bytes=64) for b in range(B)]
+        x_codes = [keep.tile([P, TOKENS], U32, name="x_codes%d" % b, align_bytes=64) for b in range(B)]
+        x_scales = [keep.tile([P, TOKENS], U8, name="x_scales%d" % b, align_bytes=64) for b in range(B)]
+        gate = [keep.tile([P, D], F32, name="gate%d" % b) for b in range(B)]
+        result = [keep.tile([P, D], F32, name="result%d" % b) for b in range(B)]
+
+        nc.vector.memset(warm[:], 0.0)
+        nc.vector.memset(w_scales[:].bitcast(I32), 0)
+        nc.vector.memset(scratch[:], 0.0)
+        make_identity(nc, ident_f32[:])
+        make_identity(nc, ident_bf16[:])
+
+        def load_scales():
+            for q in range(P // 32):
+                nc.sync.dma_start(
+                    out=w_scales[32 * q : 32 * q + 4, :].bitcast(I32),
+                    in_=gate_W_scales[0, 4 * q : 4 * q + 4, :].bitcast(I32),
+                )
 
         nc.sync.dma_start(out=x_first[:], in_=token_embeddings[0])
-        bias_col = keep.tile([P, PACK], BF16)
         nc.sync.dma_start(out=bias_col[:], in_=gate_b.rearrange("(p c) -> p c", c=PACK))
         nc.sync.dma_start(out=x_rest[:], in_=token_embeddings[1:B].rearrange("b s d -> s b d"))
         nc.sync.dma_start(out=w_words[:].bitcast(I32), in_=gate_W_words[0].bitcast(I32))
-        for q in range(P // 32):
-            nc.sync.dma_start(
-                out=w_scales[32 * q : 32 * q + 4, :].bitcast(I32),
-                in_=gate_W_scales[0, 4 * q : 4 * q + 4, :].bitcast(I32),
-            )
+        load_scales()
         nc.sync.dma_start(out=infl_sb[:], in_=splat_influences.rearrange("b s k -> s b k"))
         for h in range(B // 2):
             nc.sync.dma_start(out=dec_sb[h][:], in_=decoded[2 * h : 2 * h + 2].rearrange("b k d -> k b d"))
@@ -69,42 +79,45 @@ def tile_splatinformationflow_pb_s_kernel(
         warm_ps = psum.tile([P, P], F32, tag="bank")
         for i in range(WARM_UPS):
             nc.tensor.matmul(out=warm_ps[:], lhsT=warm[:], rhs=warm[:], start=True, stop=True)
-
         nc.scalar.activation(out=scratch[:], in_=scratch[:], func=SIGMOID)
 
-        x_codes = [keep.tile([P, TOKENS], U32, name="x_codes%d" % b, align_bytes=64) for b in range(B)]
-        x_scales = [keep.tile([P, TOKENS], U8, name="x_scales%d" % b, align_bytes=64) for b in range(B)]
+        xT = {}
+        gate_ps = {}
+        flow_ps = {}
+
+        def transpose_tokens(b):
+            x_words = x_sb[b].bitcast(F32)
+            xT[b] = psum.tile([P, WORDS, TOKENS], F32, tag="bank", name="xT%d" % b)
+            for u in range(WORDS):
+                nc.tensor.transpose(xT[b][:, u, :], x_words[:, u : D // 2 : WORDS], ident_f32[:])
+
+        def regroup_tokens(b):
+            nc.scalar.copy(
+                out=grouped[b][:].bitcast(F32).rearrange("p (s u) -> p s u", u=WORDS),
+                in_=xT[b][:].rearrange("p u s -> p s u"),
+            )
 
         def quantise_tokens(b):
-            x_words = x_sb[b].bitcast(F32)
-            xT = psum.tile([P, WORDS, TOKENS], F32, tag="bank")
+            nc.vector.quantize_mx(out=x_codes[b][:].bitcast(FP8X4), scales=x_scales[b][:], in_=grouped[b][:])
+
+        def spread_bias(engine):
+            bias_ps = psum.tile([P, WORDS, P], F32, tag="bank", name="bias_ps")
+            bias_words = bias_col[:].bitcast(F32)
             for u in range(WORDS):
-                nc.tensor.transpose(xT[:, u, :], x_words[:, u : D // 2 : WORDS], ident_f32[:])
-            grouped = keep.tile([P, TOKENS * PACK], BF16, name="grouped%d" % b, align_bytes=64)
-            nc.scalar.copy(
-                out=grouped[:].bitcast(F32).rearrange("p (s u) -> p s u", u=WORDS),
-                in_=xT[:].rearrange("p u s -> p s u"),
+                nc.tensor.transpose(bias_ps[:, u, :], bias_words[:, u : u + 1].to_broadcast([P, P]), ident_f32[:])
+            engine(
+                out=bias_all[:].bitcast(F32).rearrange("p (s u) -> p s u", u=WORDS),
+                in_=bias_ps[:].rearrange("p u s -> p s u"),
             )
-            nc.vector.quantize_mx(out=x_codes[b][:].bitcast(FP8X4), scales=x_scales[b][:], in_=grouped[:])
 
-        quantise_tokens(0)
-
-        bias_ps = psum.tile([P, WORDS, P], F32, tag="bank")
-        bias_words = bias_col[:].bitcast(F32)
-        for u in range(WORDS):
-            nc.tensor.transpose(bias_ps[:, u, :], bias_words[:, u : u + 1].to_broadcast([P, P]), ident_f32[:])
-        bias_all = keep.tile([P, D], BF16)
-        nc.scalar.copy(
-            out=bias_all[:].bitcast(F32).rearrange("p (s u) -> p s u", u=WORDS),
-            in_=bias_ps[:].rearrange("p u s -> p s u"),
-        )
-
-        for b in range(1, B):
-            quantise_tokens(b)
-
-        gate_ps = [psum.tile([P, D], F32, tag="bank", name="gate_ps%d" % b) for b in range(B)]
+        def transpose_influences():
+            inflT_ps = psum.tile([P, B, TOKENS], BF16, tag="bank", name="inflT_ps")
+            for b in range(B):
+                nc.tensor.transpose(inflT_ps[:, b, :], infl_sb[:, b, :], ident_bf16[:])
+            nc.scalar.copy(out=inflT[:], in_=inflT_ps[:])
 
         def gate_pass(b):
+            gate_ps[b] = psum.tile([P, D], F32, tag="bank", name="gate_ps%d" % b)
             nc.tensor.matmul_mx(
                 out=gate_ps[b][:],
                 lhsT=x_codes[b][:].bitcast(FP8X4),
@@ -115,27 +128,37 @@ def tile_splatinformationflow_pb_s_kernel(
                 stop=True,
             )
 
-        for b in range(B // 2):
-            gate_pass(b)
-        inflT_ps = psum.tile([P, B, TOKENS], BF16, tag="bank")
-        for b in range(B):
-            nc.tensor.transpose(inflT_ps[:, b, :], infl_sb[:, b, :], ident_bf16[:])
-        inflT = keep.tile([P, B, TOKENS], BF16)
-        nc.scalar.copy(out=inflT[:], in_=inflT_ps[:])
-        for b in range(B // 2, B):
-            gate_pass(b)
+        def add_bias(b):
+            nc.vector.tensor_add(out=gate[b][:], in0=gate_ps[b][:], in1=bias_all[:])
 
-        flow_ps = [psum.tile([P, D], F32, tag="bank", name="flow_ps%d" % b) for b in range(B)]
-        for b in range(B):
+        def sigmoid(b):
+            nc.scalar.activation(out=gate[b][:], in_=gate[b][:], func=SIGMOID)
+
+        def flow(b):
+            flow_ps[b] = psum.tile([P, D], F32, tag="bank", name="flow_ps%d" % b)
             nc.tensor.matmul(
                 out=flow_ps[b][:], lhsT=inflT[:, b, :], rhs=dec_sb[b // 2][:, b % 2, :], start=True, stop=True
             )
 
-        gate = [keep.tile([P, D], F32, name="gate%d" % b) for b in range(B)]
+        def product(b):
+            nc.vector.tensor_mul(out=result[b][:], in0=gate[b][:], in1=flow_ps[b][:])
+            nc.sync.dma_start(out=out[b], in_=result[b][:])
+
+
         for b in range(B):
-            nc.vector.tensor_add(out=gate[b][:], in0=gate_ps[b][:], in1=bias_all[:])
-            nc.scalar.activation(out=gate[b][:], in_=gate[b][:], func=SIGMOID)
+            transpose_tokens(b)
+            regroup_tokens(b)
+            quantise_tokens(b)
+        spread_bias(nc.scalar.copy)
+        for b in range(2):
+            gate_pass(b)
+        transpose_influences()
+        for b in range(2, B):
+            gate_pass(b)
         for b in range(B):
-            result = keep.tile([P, D], F32, name="result%d" % b)
-            nc.vector.tensor_mul(out=result[:], in0=gate[b][:], in1=flow_ps[b][:])
-            nc.sync.dma_start(out=out[b], in_=result[:])
+            flow(b)
+        for b in range(B):
+            add_bias(b)
+            sigmoid(b)
+        for b in range(B):
+            product(b)

@@ -114,7 +114,9 @@ def tile_splatinformationflow_pb_s_kernel(
             inflT_ps = psum.tile([P, B, TOKENS], BF16, tag="bank", name="inflT_ps")
             for b in range(B):
                 nc.tensor.transpose(inflT_ps[:, b, :], infl_sb[:, b, :], ident_bf16[:])
-            nc.scalar.copy(out=inflT[:], in_=inflT_ps[:])
+            nc.scalar.copy(
+                out=inflT[:].rearrange("p b s -> p (b s)").bitcast(F32), in_=inflT_ps[:].rearrange("p b s -> p (b s)").bitcast(F32)
+            )
 
         def gate_pass(b):
             gate_ps[b] = psum.tile([P, D], F32, tag="bank", name="gate_ps%d" % b)
@@ -152,13 +154,16 @@ def tile_splatinformationflow_pb_s_kernel(
         spread_bias(nc.scalar.copy)
         for b in range(2):
             gate_pass(b)
+        nc.scalar.copy(out=gate[0][:], in_=gate_ps[0][:])
+        nc.gpsimd.tensor_add(out=gate[0][:], in0=gate[0][:], in1=bias_all[:])
         transpose_influences()
         for b in range(2, B):
             gate_pass(b)
-        for b in range(B):
+        for b in (1, 2, 3, 0):
             flow(b)
-        for b in range(B):
+        for b in (1, 2, 3):
             add_bias(b)
             sigmoid(b)
-        for b in range(B):
+        sigmoid(0)
+        for b in (1, 2, 3, 0):
             product(b)

@@ -39,9 +39,7 @@ def tile_splatinformationflow_pb_s_kernel(
         scratch = keep.tile([P, 1], F32)
         ident_f32 = keep.tile([P, P], F32)
         ident_bf16 = keep.tile([P, P], BF16)
-        x_first = keep.tile([P, D], BF16)
-        x_rest = keep.tile([P, B - 1, D], BF16)
-        x_sb = [x_first[:]] + [x_rest[:, b - 1, :] for b in range(1, B)]
+        x_sb = [keep.tile([P, 2, D], BF16, name="x%d" % h) for h in range(B // 2)]
         infl_sb = keep.tile([P, B, SPLATS], BF16)
         w_words = keep.tile([P, 2 * D], U8, align_bytes=64)
         dec_sb = [keep.tile([P, 2, D], BF16, name="dec%d" % h) for h in range(B // 2)]
@@ -67,12 +65,14 @@ def tile_splatinformationflow_pb_s_kernel(
                     in_=gate_W_scales[0, 4 * q : 4 * q + 4, :].bitcast(I32),
                 )
 
-        nc.sync.dma_start(out=x_first[:], in_=token_embeddings[0])
+        x_rows = token_embeddings.rearrange("b s d -> (b s) d").rearrange("(h p j) d -> h p j d", h=B // 2, j=2)
+        nc.sync.dma_start(out=x_sb[0][:], in_=x_rows[0])
         nc.sync.dma_start(out=bias_col[:], in_=gate_b.rearrange("(p c) -> p c", c=PACK))
-        nc.sync.dma_start(out=x_rest[:], in_=token_embeddings[1:B].rearrange("b s d -> s b d"))
+        nc.sync.dma_start(out=x_sb[1][:], in_=x_rows[1])
         nc.sync.dma_start(out=w_words[:].bitcast(I32), in_=gate_W_words[0].bitcast(I32))
         load_scales()
-        nc.sync.dma_start(out=infl_sb[:], in_=splat_influences.rearrange("b s k -> s b k"))
+        infl_rows = splat_influences.rearrange("b s k -> (b s) k")
+        nc.sync.dma_start(out=infl_sb[:], in_=infl_rows.rearrange("(p j) k -> p j k", j=B))
         for h in range(B // 2):
             nc.sync.dma_start(out=dec_sb[h][:], in_=decoded[2 * h : 2 * h + 2].rearrange("b k d -> k b d"))
 
@@ -85,16 +85,18 @@ def tile_splatinformationflow_pb_s_kernel(
         gate_ps = {}
         flow_ps = {}
 
-        def transpose_tokens(b):
-            x_words = x_sb[b].bitcast(F32)
-            xT[b] = psum.tile([P, WORDS, TOKENS], F32, tag="bank", name="xT%d" % b)
-            for u in range(WORDS):
-                nc.tensor.transpose(xT[b][:, u, :], x_words[:, u : D // 2 : WORDS], ident_f32[:])
+        def transpose_pair(h):
+            xT[h] = psum.tile([P, 2, WORDS, P], F32, tag="bank", name="xT%d" % h)
+            for j in range(2):
+                x_words = x_sb[h][:, j, :].bitcast(F32)
+                for u in range(WORDS):
+                    nc.tensor.transpose(xT[h][:, j, u, :], x_words[:, u : D // 2 : WORDS], ident_f32[:])
 
         def regroup_tokens(b):
+            half = slice((b % 2) * TOKENS // 2, (b % 2 + 1) * TOKENS // 2)
             nc.scalar.copy(
-                out=grouped[b][:].bitcast(F32).rearrange("p (s u) -> p s u", u=WORDS),
-                in_=xT[b][:].rearrange("p u s -> p s u"),
+                out=grouped[b][:].bitcast(F32).rearrange("p (s j u) -> p s j u", j=2, u=WORDS),
+                in_=xT[b // 2][:, :, :, half].rearrange("p j u s -> p s j u"),
             )
 
         def quantise_tokens(b):
@@ -112,10 +114,11 @@ def tile_splatinformationflow_pb_s_kernel(
 
         def transpose_influences():
             inflT_ps = psum.tile([P, B, TOKENS], BF16, tag="bank", name="inflT_ps")
-            for b in range(B):
-                nc.tensor.transpose(inflT_ps[:, b, :], infl_sb[:, b, :], ident_bf16[:])
+            for j in range(B):
+                nc.tensor.transpose(inflT_ps[:, j, :], infl_sb[:, j, :], ident_bf16[:])
             nc.scalar.copy(
-                out=inflT[:].rearrange("p b s -> p (b s)").bitcast(F32), in_=inflT_ps[:].rearrange("p b s -> p (b s)").bitcast(F32)
+                out=inflT[:].rearrange("k b (s j) -> k b s j", j=B),
+                in_=inflT_ps[:].rearrange("k j (b s) -> k b s j", b=B),
             )
 
         def gate_pass(b):
@@ -148,7 +151,8 @@ def tile_splatinformationflow_pb_s_kernel(
 
 
         for b in range(B):
-            transpose_tokens(b)
+            if b % 2 == 0:
+                transpose_pair(b // 2)
             regroup_tokens(b)
             quantise_tokens(b)
         spread_bias(nc.scalar.copy)

@@ -67,10 +67,10 @@ def tile_splatinformationflow_pb_s_kernel(
 
         x_rows = token_embeddings.rearrange("b s d -> (b s) d").rearrange("(h p j) d -> h p j d", h=B // 2, j=2)
         nc.sync.dma_start(out=x_sb[0][:], in_=x_rows[0])
-        nc.sync.dma_start(out=bias_col[:], in_=gate_b.rearrange("(p c) -> p c", c=PACK))
         nc.sync.dma_start(out=x_sb[1][:], in_=x_rows[1])
         nc.sync.dma_start(out=w_words[:].bitcast(I32), in_=gate_W_words[0].bitcast(I32))
         load_scales()
+        nc.sync.dma_start(out=bias_col[:], in_=gate_b.rearrange("(p c) -> p c", c=PACK))
         infl_rows = splat_influences.rearrange("b s k -> (b s) k")
         nc.sync.dma_start(out=infl_sb[:], in_=infl_rows.rearrange("(p j) k -> p j k", j=B))
         for h in range(B // 2):

@@ -136,6 +136,10 @@ def tile_splatinformationflow_pb_s_kernel(
         def add_bias(b):
             nc.vector.tensor_add(out=gate[b][:], in0=gate_ps[b][:], in1=bias_all[:])
 
+        def add_bias_apart(b):
+            nc.scalar.copy(out=gate[b][:], in_=gate_ps[b][:])
+            nc.gpsimd.tensor_add(out=gate[b][:], in0=gate[b][:], in1=bias_all[:])
+
         def sigmoid(b):
             nc.scalar.activation(out=gate[b][:], in_=gate[b][:], func=SIGMOID)
 
@@ -149,25 +153,27 @@ def tile_splatinformationflow_pb_s_kernel(
             nc.vector.tensor_mul(out=result[b][:], in0=gate[b][:], in1=flow_ps[b][:])
             nc.sync.dma_start(out=out[b], in_=result[b][:])
 
-
+        for h in range(B // 2):
+            transpose_pair(h)
         for b in range(B):
-            if b % 2 == 0:
-                transpose_pair(b // 2)
             regroup_tokens(b)
+        for b in range(2):
             quantise_tokens(b)
-        spread_bias(nc.scalar.copy)
+        spread_bias(nc.vector.tensor_copy)
+        for b in range(2, B):
+            quantise_tokens(b)
         for b in range(2):
             gate_pass(b)
-        nc.scalar.copy(out=gate[0][:], in_=gate_ps[0][:])
-        nc.gpsimd.tensor_add(out=gate[0][:], in0=gate[0][:], in1=bias_all[:])
+        add_bias(0)
+        add_bias_apart(1)
         transpose_influences()
         for b in range(2, B):
             gate_pass(b)
-        for b in (1, 2, 3, 0):
-            flow(b)
-        for b in (1, 2, 3):
             add_bias(b)
+        order = (0, 2, 3, 1)
+        for b in order:
             sigmoid(b)
-        sigmoid(0)
-        for b in (1, 2, 3, 0):
+        for b in order:
+            flow(b)
+        for b in order:
             product(b)

@@ -20,7 +20,7 @@ SPLATS = 128
 D = 512
 WORDS = 2
 PSUM_BANKS = 8
-WARM_UPS = 4
+WARM_UP_COLUMNS = (128, 128, 128, 64)
 
 FLOPS = 2 * B * TOKENS * D * D + 2 * B * TOKENS * SPLATS * D
 
@@ -65,38 +65,35 @@ def tile_splatinformationflow_pb_s_kernel(
                     in_=gate_W_scales[0, 4 * q : 4 * q + 4, :].bitcast(I32),
                 )
 
-        x_rows = token_embeddings.rearrange("b s d -> (b s) d").rearrange("(h p j) d -> h p j d", h=B // 2, j=2)
-        nc.sync.dma_start(out=x_sb[0][:], in_=x_rows[0])
-        nc.sync.dma_start(out=x_sb[1][:], in_=x_rows[1])
+        nc.sync.dma_start(out=bias_col[:], in_=gate_b.rearrange("(p c) -> p c", c=PACK))
+        for h in range(B // 2):
+            nc.sync.dma_start(out=x_sb[h][:], in_=token_embeddings[2 * h : 2 * h + 2].rearrange("b s d -> s b d"))
         nc.sync.dma_start(out=w_words[:].bitcast(I32), in_=gate_W_words[0].bitcast(I32))
         load_scales()
-        nc.sync.dma_start(out=bias_col[:], in_=gate_b.rearrange("(p c) -> p c", c=PACK))
         infl_rows = splat_influences.rearrange("b s k -> (b s) k")
         nc.sync.dma_start(out=infl_sb[:], in_=infl_rows.rearrange("(p j) k -> p j k", j=B))
         for h in range(B // 2):
             nc.sync.dma_start(out=dec_sb[h][:], in_=decoded[2 * h : 2 * h + 2].rearrange("b k d -> k b d"))
 
         warm_ps = psum.tile([P, P], F32, tag="bank")
-        for i in range(WARM_UPS):
-            nc.tensor.matmul(out=warm_ps[:], lhsT=warm[:], rhs=warm[:], start=True, stop=True)
+        for n in WARM_UP_COLUMNS:
+            nc.tensor.matmul(out=warm_ps[:, :n], lhsT=warm[:], rhs=warm[:, :n], start=True, stop=True)
         nc.scalar.activation(out=scratch[:], in_=scratch[:], func=SIGMOID)
 
         xT = {}
         gate_ps = {}
         flow_ps = {}
 
-        def transpose_pair(h):
-            xT[h] = psum.tile([P, 2, WORDS, P], F32, tag="bank", name="xT%d" % h)
-            for j in range(2):
-                x_words = x_sb[h][:, j, :].bitcast(F32)
-                for u in range(WORDS):
-                    nc.tensor.transpose(xT[h][:, j, u, :], x_words[:, u : D // 2 : WORDS], ident_f32[:])
+        def transpose_tokens(b):
+            x_words = x_sb[b // 2][:, b % 2, :].bitcast(F32)
+            xT[b] = psum.tile([P, WORDS, TOKENS], F32, tag="bank", name="xT%d" % b)
+            for u in range(WORDS):
+                nc.tensor.transpose(xT[b][:, u, :], x_words[:, u : D // 2 : WORDS], ident_f32[:])
 
         def regroup_tokens(b):
-            half = slice((b % 2) * TOKENS // 2, (b % 2 + 1) * TOKENS // 2)
             nc.scalar.copy(
-                out=grouped[b][:].bitcast(F32).rearrange("p (s j u) -> p s j u", j=2, u=WORDS),
-                in_=xT[b // 2][:, :, :, half].rearrange("p j u s -> p s j u"),
+                out=grouped[b][:].bitcast(F32).rearrange("p (s u) -> p s u", u=WORDS),
+                in_=xT[b][:].rearrange("p u s -> p s u"),
             )
 
         def quantise_tokens(b):
@@ -153,20 +150,19 @@ def tile_splatinformationflow_pb_s_kernel(
             nc.vector.tensor_mul(out=result[b][:], in0=gate[b][:], in1=flow_ps[b][:])
             nc.sync.dma_start(out=out[b], in_=result[b][:])
 
-        for h in range(B // 2):
-            transpose_pair(h)
         for b in range(B):
+            transpose_tokens(b)
             regroup_tokens(b)
         for b in range(2):
             quantise_tokens(b)
         spread_bias(nc.vector.tensor_copy)
         for b in range(2, B):
             quantise_tokens(b)
-        for b in range(2):
-            gate_pass(b)
+        transpose_influences()
+        gate_pass(0)
+        gate_pass(1)
         add_bias(0)
         add_bias_apart(1)
-        transpose_influences()
         for b in range(2, B):
             gate_pass(b)
             add_bias(b)

@@ -20,7 +20,8 @@ SPLATS = 128
 D = 512
 WORDS = 2
 PSUM_BANKS = 8
-WARM_UP_COLUMNS = (128, 128, 128, 64)
+WARM_UPS = 3
+WARM_UP_COLUMNS = 144
 
 FLOPS = 2 * B * TOKENS * D * D + 2 * B * TOKENS * SPLATS * D
 
@@ -34,7 +35,7 @@ def tile_splatinformationflow_pb_s_kernel(
         psum = ctx.enter_context(tc.psum_pool(name="psum", bufs=PSUM_BANKS))
         ctx.enter_context(tc.manual_schedule())
 
-        warm = keep.tile([P, P], F32)
+        warm = keep.tile([P, WARM_UP_COLUMNS], F32)
         w_scales = keep.tile([P, D], U8, align_bytes=64)
         scratch = keep.tile([P, 1], F32)
         ident_f32 = keep.tile([P, P], F32)
@@ -68,16 +69,16 @@ def tile_splatinformationflow_pb_s_kernel(
         nc.sync.dma_start(out=bias_col[:], in_=gate_b.rearrange("(p c) -> p c", c=PACK))
         for h in range(B // 2):
             nc.sync.dma_start(out=x_sb[h][:], in_=token_embeddings[2 * h : 2 * h + 2].rearrange("b s d -> s b d"))
-        nc.sync.dma_start(out=w_words[:].bitcast(I32), in_=gate_W_words[0].bitcast(I32))
-        load_scales()
         infl_rows = splat_influences.rearrange("b s k -> (b s) k")
         nc.sync.dma_start(out=infl_sb[:], in_=infl_rows.rearrange("(p j) k -> p j k", j=B))
+        nc.sync.dma_start(out=w_words[:].bitcast(I32), in_=gate_W_words[0].bitcast(I32))
+        load_scales()
         for h in range(B // 2):
             nc.sync.dma_start(out=dec_sb[h][:], in_=decoded[2 * h : 2 * h + 2].rearrange("b k d -> k b d"))
 
-        warm_ps = psum.tile([P, P], F32, tag="bank")
-        for n in WARM_UP_COLUMNS:
-            nc.tensor.matmul(out=warm_ps[:, :n], lhsT=warm[:], rhs=warm[:, :n], start=True, stop=True)
+        warm_ps = psum.tile([P, WARM_UP_COLUMNS], F32, tag="bank")
+        for i in range(WARM_UPS):
+            nc.tensor.matmul(out=warm_ps[:], lhsT=warm[:, :P], rhs=warm[:], start=True, stop=True)
         nc.scalar.activation(out=scratch[:], in_=scratch[:], func=SIGMOID)
 
         xT = {}
@@ -153,11 +154,9 @@ def tile_splatinformationflow_pb_s_kernel(
         for b in range(B):
             transpose_tokens(b)
             regroup_tokens(b)
-        for b in range(2):
+        for b in range(B):
             quantise_tokens(b)
-        spread_bias(nc.vector.tensor_copy)
-        for b in range(2, B):
-            quantise_tokens(b)
+        spread_bias(nc.scalar.copy)
         transpose_influences()
         gate_pass(0)
         gate_pass(1)

@@ -147,9 +147,11 @@ def tile_splatinformationflow_pb_s_kernel(
                 out=flow_ps[b][:], lhsT=inflT[:, b, :], rhs=dec_sb[b // 2][:, b % 2, :], start=True, stop=True
             )
 
-        def product(b):
-            nc.vector.tensor_mul(out=result[b][:], in0=gate[b][:], in1=flow_ps[b][:])
-            nc.sync.dma_start(out=out[b], in_=result[b][:])
+        def product(b, pieces):
+            for i in range(pieces):
+                cols = slice(i * D // pieces, (i + 1) * D // pieces)
+                nc.vector.tensor_mul(out=result[b][:, cols], in0=gate[b][:, cols], in1=flow_ps[b][:, cols])
+                nc.sync.dma_start(out=out[b, :, cols], in_=result[b][:, cols])
 
         for b in range(B):
             transpose_tokens(b)
@@ -171,4 +173,4 @@ def tile_splatinformationflow_pb_s_kernel(
         for b in order:
             flow(b)
         for b in order:
-            product(b)
+            product(b, 2 if b == order[0] else 1)

@@ -20,8 +20,8 @@ SPLATS = 128
 D = 512
 WORDS = 2
 PSUM_BANKS = 8
-WARM_UPS = 3
-WARM_UP_COLUMNS = 144
+WARM_UPS = 2
+WARM_UP_COLUMNS = 224
 
 FLOPS = 2 * B * TOKENS * D * D + 2 * B * TOKENS * SPLATS * D
 
@@ -153,12 +153,12 @@ def tile_splatinformationflow_pb_s_kernel(
                 nc.vector.tensor_mul(out=result[b][:, cols], in0=gate[b][:, cols], in1=flow_ps[b][:, cols])
                 nc.sync.dma_start(out=out[b, :, cols], in_=result[b][:, cols])
 
+        spread_bias(nc.vector.tensor_copy)
         for b in range(B):
             transpose_tokens(b)
             regroup_tokens(b)
         for b in range(B):
             quantise_tokens(b)
-        spread_bias(nc.scalar.copy)
         transpose_influences()
         gate_pass(0)
         gate_pass(1)

from contextlib import ExitStack

import concourse.mybir as mybir
from concourse.masks import make_identity

F32 = mybir.dt.float32
BF16 = mybir.dt.bfloat16
I32 = mybir.dt.int32
U32 = mybir.dt.uint32
U8 = mybir.dt.uint8
FP8X4 = mybir.dt.float8_e4m3fn_x4
FP4X4 = mybir.dt.float4_e2m1fn_x4
SIGMOID = mybir.ActivationFunctionType.Sigmoid

P = 128
PACK = 4
B = 4
TOKENS = 128
SPLATS = 128
D = 512
WORDS = 2
PSUM_BANKS = 8
WARM_UPS = 2
WARM_UP_COLUMNS = 224

FLOPS = 2 * B * TOKENS * D * D + 2 * B * TOKENS * SPLATS * D


def tile_splatinformationflow_pb_s_kernel(
    tc, token_embeddings, splat_influences, decoded, gate_W_words, gate_W_scales, gate_b, out
):
    nc = tc.nc
    with ExitStack() as ctx:
        keep = ctx.enter_context(tc.tile_pool(name="keep", bufs=1))
        psum = ctx.enter_context(tc.psum_pool(name="psum", bufs=PSUM_BANKS))
        ctx.enter_context(tc.manual_schedule())

        warm = keep.tile([P, WARM_UP_COLUMNS], F32)
        w_scales = keep.tile([P, D], U8, align_bytes=64)
        scratch = keep.tile([P, 1], F32)
        ident_f32 = keep.tile([P, P], F32)
        ident_bf16 = keep.tile([P, P], BF16)
        x_sb = [keep.tile([P, 2, D], BF16, name="x%d" % h) for h in range(B // 2)]
        infl_sb = keep.tile([P, B, SPLATS], BF16)
        w_words = keep.tile([P, 2 * D], U8, align_bytes=64)
        dec_sb = [keep.tile([P, 2, D], BF16, name="dec%d" % h) for h in range(B // 2)]
        bias_col = keep.tile([P, PACK], BF16)
        bias_all = keep.tile([P, D], BF16)
        inflT = keep.tile([P, B, TOKENS], BF16)
        grouped = [keep.tile([P, TOKENS * PACK], BF16, name="grouped%d" % b, align_bytes=64) for b in range(B)]
        x_codes = [keep.tile([P, TOKENS], U32, name="x_codes%d" % b, align_bytes=64) for b in range(B)]
        x_scales = [keep.tile([P, TOKENS], U8, name="x_scales%d" % b, align_bytes=64) for b in range(B)]
        gate = [keep.tile([P, D], F32, name="gate%d" % b) for b in range(B)]
        result = [keep.tile([P, D], F32, name="result%d" % b) for b in range(B)]

        nc.vector.memset(warm[:], 0.0)
        nc.vector.memset(w_scales[:].bitcast(I32), 0)
        nc.vector.memset(scratch[:], 0.0)
        make_identity(nc, ident_f32[:])
        make_identity(nc, ident_bf16[:])

        def load_scales():
            for q in range(P // 32):
                nc.sync.dma_start(
                    out=w_scales[32 * q : 32 * q + 4, :].bitcast(I32),
                    in_=gate_W_scales[0, 4 * q : 4 * q + 4, :].bitcast(I32),
                )

        nc.sync.dma_start(out=bias_col[:], in_=gate_b.rearrange("(p c) -> p c", c=PACK))
        for h in range(B // 2):
            nc.sync.dma_start(out=x_sb[h][:], in_=token_embeddings[2 * h : 2 * h + 2].rearrange("b s d -> s b d"))
        infl_rows = splat_influences.rearrange("b s k -> (b s) k")
        nc.sync.dma_start(out=infl_sb[:], in_=infl_rows.rearrange("(p j) k -> p j k", j=B))
        nc.sync.dma_start(out=w_words[:].bitcast(I32), in_=gate_W_words[0].bitcast(I32))
        load_scales()
        for h in range(B // 2):
            nc.sync.dma_start(out=dec_sb[h][:], in_=decoded[2 * h : 2 * h + 2].rearrange("b k d -> k b d"))

        warm_ps = psum.tile([P, WARM_UP_COLUMNS], F32, tag="bank")
        for i in range(WARM_UPS):
            nc.tensor.matmul(out=warm_ps[:], lhsT=warm[:, :P], rhs=warm[:], start=True, stop=True)
        nc.scalar.activation(out=scratch[:], in_=scratch[:], func=SIGMOID)

        xT = {}
        gate_ps = {}
        flow_ps = {}

        def transpose_tokens(b):
            x_words = x_sb[b // 2][:, b % 2, :].bitcast(F32)
            xT[b] = psum.tile([P, WORDS, TOKENS], F32, tag="bank", name="xT%d" % b)
            for u in range(WORDS):
                nc.tensor.transpose(xT[b][:, u, :], x_words[:, u : D // 2 : WORDS], ident_f32[:])

        def regroup_tokens(b):
            nc.scalar.copy(
                out=grouped[b][:].bitcast(F32).rearrange("p (s u) -> p s u", u=WORDS),
                in_=xT[b][:].rearrange("p u s -> p s u"),
            )

        def quantise_tokens(b):
            nc.vector.quantize_mx(out=x_codes[b][:].bitcast(FP8X4), scales=x_scales[b][:], in_=grouped[b][:])

        def spread_bias(engine):
            bias_ps = psum.tile([P, WORDS, P], F32, tag="bank", name="bias_ps")
            bias_words = bias_col[:].bitcast(F32)
            for u in range(WORDS):
                nc.tensor.transpose(bias_ps[:, u, :], bias_words[:, u : u + 1].to_broadcast([P, P]), ident_f32[:])
            engine(
                out=bias_all[:].bitcast(F32).rearrange("p (s u) -> p s u", u=WORDS),
                in_=bias_ps[:].rearrange("p u s -> p s u"),
            )

        def transpose_influences():
            inflT_ps = psum.tile([P, B, TOKENS], BF16, tag="bank", name="inflT_ps")
            for j in range(B):
                nc.tensor.transpose(inflT_ps[:, j, :], infl_sb[:, j, :], ident_bf16[:])
            nc.scalar.copy(
                out=inflT[:].rearrange("k b (s j) -> k b s j", j=B),
                in_=inflT_ps[:].rearrange("k j (b s) -> k b s j", b=B),
            )

        def gate_pass(b):
            gate_ps[b] = psum.tile([P, D], F32, tag="bank", name="gate_ps%d" % b)
            nc.tensor.matmul_mx(
                out=gate_ps[b][:],
                lhsT=x_codes[b][:].bitcast(FP8X4),
                lhsT_scale=x_scales[b][:],
                rhs=w_words[:].bitcast(FP4X4),
                rhs_scale=w_scales[:],
                start=True,
                stop=True,
            )

        def add_bias(b):
            nc.vector.tensor_add(out=gate[b][:], in0=gate_ps[b][:], in1=bias_all[:])

        def add_bias_apart(b):
            nc.scalar.copy(out=gate[b][:], in_=gate_ps[b][:])
            nc.gpsimd.tensor_add(out=gate[b][:], in0=gate[b][:], in1=bias_all[:])

        def sigmoid(b):
            nc.scalar.activation(out=gate[b][:], in_=gate[b][:], func=SIGMOID)

        def flow(b):
            flow_ps[b] = psum.tile([P, D], F32, tag="bank", name="flow_ps%d" % b)
            nc.tensor.matmul(
                out=flow_ps[b][:], lhsT=inflT[:, b, :], rhs=dec_sb[b // 2][:, b % 2, :], start=True, stop=True
            )

        def product(b, pieces):
            for i in range(pieces):
                cols = slice(i * D // pieces, (i + 1) * D // pieces)
                nc.vector.tensor_mul(out=result[b][:, cols], in0=gate[b][:, cols], in1=flow_ps[b][:, cols])
                nc.sync.dma_start(out=out[b, :, cols], in_=result[b][:, cols])

        spread_bias(nc.vector.tensor_copy)
        for b in range(B):
            transpose_tokens(b)
            regroup_tokens(b)
        for b in range(B):
            quantise_tokens(b)
        transpose_influences()
        gate_pass(0)
        gate_pass(1)
        add_bias(0)
        add_bias_apart(1)
        for b in range(2, B):
            gate_pass(b)
            add_bias(b)
        order = (0, 2, 3, 1)
        for b in order:
            sigmoid(b)
        for b in order:
            flow(b)
        for b in order:
            product(b, 2 if b == order[0] else 1)
